import numpy as np
import ml_dtypes

BF16 = ml_dtypes.bfloat16


def bf(x):
    return np.asarray(x, np.float32).astype(BF16)


def f32(x):
    return np.asarray(x, np.float32)


def f64(x):
    return np.asarray(x).astype(np.float64)


def striped(idx):
    return np.tile(idx.reshape(-1, 16).T, (8, 1))


S, D, R, M, N = 2048, 128, 128, 512, 512


def setup_inputs():
    return {"table": bf(np.random.standard_normal((S, D))), "w": bf(np.random.standard_normal((D, M)) / np.sqrt(D)), "lf": bf(np.random.standard_normal((D, R)) / np.sqrt(D)), "ls": bf(0.5 * np.random.standard_normal((R, M)) / np.sqrt(R)), "offs": striped(np.random.permutation(S)[:N])}


def reference(table, w, lf, ls, offs):
    idx = offs[:16].T.reshape(-1)
    picked = f64(table)[idx].T
    h = f64(lf).T @ picked
    return f64(w).T @ picked + f64(ls).T @ h

@@ -1,0 +1,74 @@
+import concourse.masks as masks
+import concourse.mybir as mybir
+
+BF16 = mybir.dt.bfloat16
+F32 = mybir.dt.float32
+U16 = mybir.dt.uint16
+
+P = 128
+S, D, R, M, N = 2048, 128, 128, 512, 512
+BLOCKS = S // P
+BLOCKS_PER_LOAD = 4
+LOADS = BLOCKS // BLOCKS_PER_LOAD
+GROUPS = M // P
+
+FLOPS = 2 * N * (D * M + D * R + R * M)
+
+
+def tile_generalizedmatrix_kernel(tc, table, w, lf, ls, offs, out):
+    nc = tc.nc
+    with (
+        tc.tile_pool(name="held", bufs=1) as held,
+        tc.tile_pool(name="results", bufs=GROUPS) as results,
+        tc.psum_pool(name="flips", bufs=2) as flips,
+        tc.psum_pool(name="sums", bufs=1) as sums,
+    ):
+        offsets = held.tile([P, N // 16], U16, name="offsets")
+        nc.sync.dma_start(offsets[:], offs)
+
+        table_blocks = table.rearrange("(b p) d -> p b d", p=P)
+        rows = [held.tile([P, BLOCKS_PER_LOAD, D], BF16, name=f"rows{c}") for c in range(LOADS)]
+        for c in range(LOADS):
+            queue = nc.sync if c % 2 == 0 else nc.scalar
+            queue.dma_start(rows[c][:], table_blocks[:, c * BLOCKS_PER_LOAD : (c + 1) * BLOCKS_PER_LOAD, :])
+
+        lf_sb = held.tile([D, R], BF16, name="lf_sb")
+        w_sb = held.tile([D, M], BF16, name="w_sb")
+        ls_sb = held.tile([R, M], BF16, name="ls_sb")
+        nc.sync.dma_start(lf_sb[:], lf)
+        nc.sync.dma_start(w_sb[:], w)
+        nc.scalar.dma_start(ls_sb[:], ls)
+
+        identity = held.tile([P, P], BF16, name="identity")
+        masks.make_identity(nc, identity[:])
+
+        window = held.tile([D, S], BF16, name="window")
+        for c in range(LOADS):
+            flipped = flips.tile([D, BLOCKS_PER_LOAD * P], BF16, name="flipped")
+            for k in range(BLOCKS_PER_LOAD):
+                nc.tensor.transpose(flipped[:, k * P : (k + 1) * P], rows[c][:, k, :], identity[:])
+            columns = window[:, c * BLOCKS_PER_LOAD * P : (c + 1) * BLOCKS_PER_LOAD * P]
+            if c % 2 == 0:
+                nc.vector.tensor_copy(columns, flipped[:])
+            else:
+                nc.scalar.copy(columns, flipped[:])
+
+        h_sum = sums.tile([R, N], F32, name="h_sum")
+        nc.tensor.matmul(h_sum[:], lf_sb[:], window[:].indirect(offsets[:]), start=True, stop=True)
+        out_sums = [sums.tile([P, N], F32, name=f"out_sum{g}") for g in range(GROUPS)]
+        for g in range(GROUPS):
+            nc.tensor.matmul(
+                out_sums[g][:], w_sb[:, g * P : (g + 1) * P], window[:].indirect(offsets[:]), start=True, stop=False
+            )
+
+        h_sb = held.tile([R, N], BF16, name="h_sb")
+        nc.vector.tensor_copy(h_sb[:], h_sum[:])
+
+        for g in range(GROUPS):
+            nc.tensor.matmul(out_sums[g][:], ls_sb[:, g * P : (g + 1) * P], h_sb[:], start=False, stop=True)
+            result = results.tile([P, N], F32, name="result")
+            if g % 2 == 0:
+                nc.vector.tensor_copy(result[:], out_sums[g][:])
+            else:
+                nc.scalar.copy(result[:], out_sums[g][:])
+            nc.sync.dma_start(out[g * P : (g + 1) * P, :], result[:])

@@ -55,16 +55,20 @@ def tile_generalizedmatrix_kernel(tc, table, w, lf, ls, offs, out):
 
         h_sum = sums.tile([R, N], F32, name="h_sum")
         nc.tensor.matmul(h_sum[:], lf_sb[:], window[:].indirect(offsets[:]), start=True, stop=True)
+        h_sb = held.tile([R, N], BF16, name="h_sb")
+        nc.vector.tensor_copy(h_sb[:], h_sum[:])
+
         out_sums = [sums.tile([P, N], F32, name=f"out_sum{g}") for g in range(GROUPS)]
-        for g in range(GROUPS):
+
+        def open_group(g):
             nc.tensor.matmul(
                 out_sums[g][:], w_sb[:, g * P : (g + 1) * P], window[:].indirect(offsets[:]), start=True, stop=False
             )
 
-        h_sb = held.tile([R, N], BF16, name="h_sb")
-        nc.vector.tensor_copy(h_sb[:], h_sum[:])
-
+        open_group(0)
         for g in range(GROUPS):
+            if g + 1 < GROUPS:
+                open_group(g + 1)
             nc.tensor.matmul(out_sums[g][:], ls_sb[:, g * P : (g + 1) * P], h_sb[:], start=False, stop=True)
             result = results.tile([P, N], F32, name="result")
             if g % 2 == 0:

@@ -10,6 +10,7 @@ S, D, R, M, N = 2048, 128, 128, 512, 512
 BLOCKS = S // P
 BLOCKS_PER_LOAD = 4
 LOADS = BLOCKS // BLOCKS_PER_LOAD
+WARMING_MATMULS = 4
 GROUPS = M // P
 
 FLOPS = 2 * N * (D * M + D * R + R * M)
@@ -42,6 +43,12 @@ def tile_generalizedmatrix_kernel(tc, table, w, lf, ls, offs, out):
         identity = held.tile([P, P], BF16, name="identity")
         masks.make_identity(nc, identity[:])
 
+        zeros = held.tile([P, N], BF16, name="zeros")
+        nc.vector.memset(zeros[:], 0.0)
+        unused = sums.tile([P, N], F32, name="unused")
+        for i in range(WARMING_MATMULS):
+            nc.tensor.matmul(unused[:], zeros[:, :P], zeros[:], start=True, stop=True)
+
         window = held.tile([D, S], BF16, name="window")
         for c in range(LOADS):
             flipped = flips.tile([D, BLOCKS_PER_LOAD * P], BF16, name="flipped")
@@ -52,23 +59,20 @@ def tile_generalizedmatrix_kernel(tc, table, w, lf, ls, offs, out):
                 nc.vector.tensor_copy(columns, flipped[:])
             else:
                 nc.scalar.copy(columns, flipped[:])
+            nc.tensor.matmul(unused[:], rows[c][:, 0, :], rows[c][:], start=True, stop=True)
 
         h_sum = sums.tile([R, N], F32, name="h_sum")
         nc.tensor.matmul(h_sum[:], lf_sb[:], window[:].indirect(offsets[:]), start=True, stop=True)
-        h_sb = held.tile([R, N], BF16, name="h_sb")
-        nc.vector.tensor_copy(h_sb[:], h_sum[:])
-
         out_sums = [sums.tile([P, N], F32, name=f"out_sum{g}") for g in range(GROUPS)]
-
-        def open_group(g):
+        for g in range(GROUPS):
             nc.tensor.matmul(
                 out_sums[g][:], w_sb[:, g * P : (g + 1) * P], window[:].indirect(offsets[:]), start=True, stop=False
             )
 
-        open_group(0)
+        h_sb = held.tile([R, N], BF16, name="h_sb")
+        nc.vector.tensor_copy(h_sb[:], h_sum[:])
+
         for g in range(GROUPS):
-            if g + 1 < GROUPS:
-                open_group(g + 1)
             nc.tensor.matmul(out_sums[g][:], ls_sb[:, g * P : (g + 1) * P], h_sb[:], start=False, stop=True)
             result = results.tile([P, N], F32, name="result")
             if g % 2 == 0:

@@ -10,7 +10,6 @@ S, D, R, M, N = 2048, 128, 128, 512, 512
 BLOCKS = S // P
 BLOCKS_PER_LOAD = 4
 LOADS = BLOCKS // BLOCKS_PER_LOAD
-WARMING_MATMULS = 4
 GROUPS = M // P
 
 FLOPS = 2 * N * (D * M + D * R + R * M)
@@ -27,11 +26,11 @@ def tile_generalizedmatrix_kernel(tc, table, w, lf, ls, offs, out):
         offsets = held.tile([P, N // 16], U16, name="offsets")
         nc.sync.dma_start(offsets[:], offs)
 
-        table_blocks = table.rearrange("(b p) d -> p b d", p=P)
+        table_runs = table.rearrange("(c p e) d -> c p e d", p=P, e=BLOCKS_PER_LOAD)
         rows = [held.tile([P, BLOCKS_PER_LOAD, D], BF16, name=f"rows{c}") for c in range(LOADS)]
         for c in range(LOADS):
             queue = nc.sync if c % 2 == 0 else nc.scalar
-            queue.dma_start(rows[c][:], table_blocks[:, c * BLOCKS_PER_LOAD : (c + 1) * BLOCKS_PER_LOAD, :])
+            queue.dma_start(rows[c][:], table_runs[c])
 
         lf_sb = held.tile([D, R], BF16, name="lf_sb")
         w_sb = held.tile([D, M], BF16, name="w_sb")
@@ -43,23 +42,18 @@ def tile_generalizedmatrix_kernel(tc, table, w, lf, ls, offs, out):
         identity = held.tile([P, P], BF16, name="identity")
         masks.make_identity(nc, identity[:])
 
-        zeros = held.tile([P, N], BF16, name="zeros")
-        nc.vector.memset(zeros[:], 0.0)
-        unused = sums.tile([P, N], F32, name="unused")
-        for i in range(WARMING_MATMULS):
-            nc.tensor.matmul(unused[:], zeros[:, :P], zeros[:], start=True, stop=True)
-
         window = held.tile([D, S], BF16, name="window")
         for c in range(LOADS):
             flipped = flips.tile([D, BLOCKS_PER_LOAD * P], BF16, name="flipped")
             for k in range(BLOCKS_PER_LOAD):
                 nc.tensor.transpose(flipped[:, k * P : (k + 1) * P], rows[c][:, k, :], identity[:])
             columns = window[:, c * BLOCKS_PER_LOAD * P : (c + 1) * BLOCKS_PER_LOAD * P]
+            columns = columns.rearrange("d (p e) -> d p e", e=BLOCKS_PER_LOAD)
+            in_order = flipped[:].rearrange("d (e p) -> d p e", e=BLOCKS_PER_LOAD)
             if c % 2 == 0:
-                nc.vector.tensor_copy(columns, flipped[:])
+                nc.vector.tensor_copy(columns, in_order)
             else:
-                nc.scalar.copy(columns, flipped[:])
-            nc.tensor.matmul(unused[:], rows[c][:, 0, :], rows[c][:], start=True, stop=True)
+                nc.scalar.copy(columns, in_order)
 
         h_sum = sums.tile([R, N], F32, name="h_sum")
         nc.tensor.matmul(h_sum[:], lf_sb[:], window[:].indirect(offsets[:]), start=True, stop=True)

@@ -10,6 +10,7 @@ S, D, R, M, N = 2048, 128, 128, 512, 512
 BLOCKS = S // P
 BLOCKS_PER_LOAD = 4
 LOADS = BLOCKS // BLOCKS_PER_LOAD
+WARMING_MATMULS = 4
 GROUPS = M // P
 
 FLOPS = 2 * N * (D * M + D * R + R * M)
@@ -26,11 +27,11 @@ def tile_generalizedmatrix_kernel(tc, table, w, lf, ls, offs, out):
         offsets = held.tile([P, N // 16], U16, name="offsets")
         nc.sync.dma_start(offsets[:], offs)
 
-        table_runs = table.rearrange("(c p e) d -> c p e d", p=P, e=BLOCKS_PER_LOAD)
+        table_blocks = table.rearrange("(b p) d -> p b d", p=P)
         rows = [held.tile([P, BLOCKS_PER_LOAD, D], BF16, name=f"rows{c}") for c in range(LOADS)]
         for c in range(LOADS):
             queue = nc.sync if c % 2 == 0 else nc.scalar
-            queue.dma_start(rows[c][:], table_runs[c])
+            queue.dma_start(rows[c][:], table_blocks[:, c * BLOCKS_PER_LOAD : (c + 1) * BLOCKS_PER_LOAD, :])
 
         lf_sb = held.tile([D, R], BF16, name="lf_sb")
         w_sb = held.tile([D, M], BF16, name="w_sb")
@@ -42,18 +43,22 @@ def tile_generalizedmatrix_kernel(tc, table, w, lf, ls, offs, out):
         identity = held.tile([P, P], BF16, name="identity")
         masks.make_identity(nc, identity[:])
 
+        zeros = held.tile([P, N], BF16, name="zeros")
+        nc.vector.memset(zeros[:], 0.0)
+        unused = sums.tile([P, N], F32, name="unused")
+        for i in range(WARMING_MATMULS):
+            nc.tensor.matmul(unused[:], zeros[:, :P], zeros[:], start=True, stop=True)
+
         window = held.tile([D, S], BF16, name="window")
         for c in range(LOADS):
             flipped = flips.tile([D, BLOCKS_PER_LOAD * P], BF16, name="flipped")
             for k in range(BLOCKS_PER_LOAD):
                 nc.tensor.transpose(flipped[:, k * P : (k + 1) * P], rows[c][:, k, :], identity[:])
             columns = window[:, c * BLOCKS_PER_LOAD * P : (c + 1) * BLOCKS_PER_LOAD * P]
-            columns = columns.rearrange("d (p e) -> d p e", e=BLOCKS_PER_LOAD)
-            in_order = flipped[:].rearrange("d (e p) -> d p e", e=BLOCKS_PER_LOAD)
             if c % 2 == 0:
-                nc.vector.tensor_copy(columns, in_order)
+                nc.vector.tensor_copy(columns, flipped[:])
             else:
-                nc.scalar.copy(columns, in_order)
+                nc.scalar.copy(columns, flipped[:])
 
         h_sum = sums.tile([R, N], F32, name="h_sum")
         nc.tensor.matmul(h_sum[:], lf_sb[:], window[:].indirect(offsets[:]), start=True, stop=True)

@@ -8,9 +8,8 @@ U16 = mybir.dt.uint16
 P = 128
 S, D, R, M, N = 2048, 128, 128, 512, 512
 BLOCKS = S // P
-BLOCKS_PER_LOAD = 4
+BLOCKS_PER_LOAD = 2
 LOADS = BLOCKS // BLOCKS_PER_LOAD
-WARMING_MATMULS = 4
 GROUPS = M // P
 
 FLOPS = 2 * N * (D * M + D * R + R * M)
@@ -42,12 +41,6 @@ def tile_generalizedmatrix_kernel(tc, table, w, lf, ls, offs, out):
 
         identity = held.tile([P, P], BF16, name="identity")
         masks.make_identity(nc, identity[:])
-
-        zeros = held.tile([P, N], BF16, name="zeros")
-        nc.vector.memset(zeros[:], 0.0)
-        unused = sums.tile([P, N], F32, name="unused")
-        for i in range(WARMING_MATMULS):
-            nc.tensor.matmul(unused[:], zeros[:, :P], zeros[:], start=True, stop=True)
 
         window = held.tile([D, S], BF16, name="window")
         for c in range(LOADS):

@@ -8,8 +8,9 @@ U16 = mybir.dt.uint16
 P = 128
 S, D, R, M, N = 2048, 128, 128, 512, 512
 BLOCKS = S // P
-BLOCKS_PER_LOAD = 2
+BLOCKS_PER_LOAD = 4
 LOADS = BLOCKS // BLOCKS_PER_LOAD
+WARMING_MATMULS = 4
 GROUPS = M // P
 
 FLOPS = 2 * N * (D * M + D * R + R * M)
@@ -20,8 +21,7 @@ def tile_generalizedmatrix_kernel(tc, table, w, lf, ls, offs, out):
     with (
         tc.tile_pool(name="held", bufs=1) as held,
         tc.tile_pool(name="results", bufs=GROUPS) as results,
-        tc.psum_pool(name="flips", bufs=2) as flips,
-        tc.psum_pool(name="sums", bufs=1) as sums,
+        tc.psum_pool(name="warming", bufs=1) as warming,
     ):
         offsets = held.tile([P, N // 16], U16, name="offsets")
         nc.sync.dma_start(offsets[:], offs)
@@ -42,33 +42,41 @@ def tile_generalizedmatrix_kernel(tc, table, w, lf, ls, offs, out):
         identity = held.tile([P, P], BF16, name="identity")
         masks.make_identity(nc, identity[:])
 
+        zeros = held.tile([P, N], BF16, name="zeros")
+        nc.vector.memset(zeros[:], 0.0)
+        unused = warming.tile([P, N], F32, name="unused")
+        for i in range(WARMING_MATMULS):
+            nc.tensor.matmul(unused[:], zeros[:, :P], zeros[:], start=True, stop=True)
+
         window = held.tile([D, S], BF16, name="window")
-        for c in range(LOADS):
-            flipped = flips.tile([D, BLOCKS_PER_LOAD * P], BF16, name="flipped")
-            for k in range(BLOCKS_PER_LOAD):
-                nc.tensor.transpose(flipped[:, k * P : (k + 1) * P], rows[c][:, k, :], identity[:])
-            columns = window[:, c * BLOCKS_PER_LOAD * P : (c + 1) * BLOCKS_PER_LOAD * P]
-            if c % 2 == 0:
-                nc.vector.tensor_copy(columns, flipped[:])
-            else:
-                nc.scalar.copy(columns, flipped[:])
+        with tc.psum_pool(name="flips", bufs=LOADS) as flips:
+            for c in range(LOADS):
+                flipped = flips.tile([D, BLOCKS_PER_LOAD * P], BF16, name="flipped")
+                for k in range(BLOCKS_PER_LOAD):
+                    nc.tensor.transpose(flipped[:, k * P : (k + 1) * P], rows[c][:, k, :], identity[:])
+                columns = window[:, c * BLOCKS_PER_LOAD * P : (c + 1) * BLOCKS_PER_LOAD * P]
+                if c % 2 == 0:
+                    nc.vector.tensor_copy(columns, flipped[:])
+                else:
+                    nc.scalar.copy(columns, flipped[:])
 
-        h_sum = sums.tile([R, N], F32, name="h_sum")
-        nc.tensor.matmul(h_sum[:], lf_sb[:], window[:].indirect(offsets[:]), start=True, stop=True)
-        out_sums = [sums.tile([P, N], F32, name=f"out_sum{g}") for g in range(GROUPS)]
-        for g in range(GROUPS):
-            nc.tensor.matmul(
-                out_sums[g][:], w_sb[:, g * P : (g + 1) * P], window[:].indirect(offsets[:]), start=True, stop=False
-            )
+        with tc.psum_pool(name="sums", bufs=1) as sums:
+            h_sum = sums.tile([R, N], F32, name="h_sum")
+            nc.tensor.matmul(h_sum[:], lf_sb[:], window[:].indirect(offsets[:]), start=True, stop=True)
+            out_sums = [sums.tile([P, N], F32, name=f"out_sum{g}") for g in range(GROUPS)]
+            for g in range(GROUPS):
+                nc.tensor.matmul(
+                    out_sums[g][:], w_sb[:, g * P : (g + 1) * P], window[:].indirect(offsets[:]), start=True, stop=False
+                )
 
-        h_sb = held.tile([R, N], BF16, name="h_sb")
-        nc.vector.tensor_copy(h_sb[:], h_sum[:])
+            h_sb = held.tile([R, N], BF16, name="h_sb")
+            nc.vector.tensor_copy(h_sb[:], h_sum[:])
 
-        for g in range(GROUPS):
-            nc.tensor.matmul(out_sums[g][:], ls_sb[:, g * P : (g + 1) * P], h_sb[:], start=False, stop=True)
-            result = results.tile([P, N], F32, name="result")
-            if g % 2 == 0:
-                nc.vector.tensor_copy(result[:], out_sums[g][:])
-            else:
-                nc.scalar.copy(result[:], out_sums[g][:])
-            nc.sync.dma_start(out[g * P : (g + 1) * P, :], result[:])
+            for g in range(GROUPS):
+                nc.tensor.matmul(out_sums[g][:], ls_sb[:, g * P : (g + 1) * P], h_sb[:], start=False, stop=True)
+                result = results.tile([P, N], F32, name="result")
+                if g % 2 == 0:
+                    nc.vector.tensor_copy(result[:], out_sums[g][:])
+                else:
+                    nc.scalar.copy(result[:], out_sums[g][:])
+                nc.sync.dma_start(out[g * P : (g + 1) * P, :], result[:])

@@ -20,17 +20,17 @@ def tile_generalizedmatrix_kernel(tc, table, w, lf, ls, offs, out):
     nc = tc.nc
     with (
         tc.tile_pool(name="held", bufs=1) as held,
-        tc.tile_pool(name="results", bufs=GROUPS) as results,
+        tc.tile_pool(name="results", bufs=2 * GROUPS) as results,
         tc.psum_pool(name="warming", bufs=1) as warming,
     ):
-        offsets = held.tile([P, N // 16], U16, name="offsets")
-        nc.sync.dma_start(offsets[:], offs)
-
         table_blocks = table.rearrange("(b p) d -> p b d", p=P)
         rows = [held.tile([P, BLOCKS_PER_LOAD, D], BF16, name=f"rows{c}") for c in range(LOADS)]
         for c in range(LOADS):
             queue = nc.sync if c % 2 == 0 else nc.scalar
             queue.dma_start(rows[c][:], table_blocks[:, c * BLOCKS_PER_LOAD : (c + 1) * BLOCKS_PER_LOAD, :])
+
+        offsets = held.tile([P, N // 16], U16, name="offsets")
+        nc.sync.dma_start(offsets[:], offs)
 
         lf_sb = held.tile([D, R], BF16, name="lf_sb")
         w_sb = held.tile([D, M], BF16, name="w_sb")
@@ -74,9 +74,11 @@ def tile_generalizedmatrix_kernel(tc, table, w, lf, ls, offs, out):
 
             for g in range(GROUPS):
                 nc.tensor.matmul(out_sums[g][:], ls_sb[:, g * P : (g + 1) * P], h_sb[:], start=False, stop=True)
-                result = results.tile([P, N], F32, name="result")
-                if g % 2 == 0:
-                    nc.vector.tensor_copy(result[:], out_sums[g][:])
-                else:
-                    nc.scalar.copy(result[:], out_sums[g][:])
-                nc.sync.dma_start(out[g * P : (g + 1) * P, :], result[:])
+                for half in range(2):
+                    columns = slice(half * N // 2, (half + 1) * N // 2)
+                    result = results.tile([P, N // 2], F32, name="result")
+                    if g % 2 == 0:
+                        nc.vector.tensor_copy(result[:], out_sums[g][:, columns])
+                    else:
+                        nc.scalar.copy(result[:], out_sums[g][:, columns])
+                    nc.sync.dma_start(out[g * P : (g + 1) * P, columns], result[:])

import concourse.masks as masks
import concourse.mybir as mybir

BF16 = mybir.dt.bfloat16
F32 = mybir.dt.float32
U16 = mybir.dt.uint16

P = 128
S, D, R, M, N = 2048, 128, 128, 512, 512
BLOCKS = S // P
BLOCKS_PER_LOAD = 4
LOADS = BLOCKS // BLOCKS_PER_LOAD
WARMING_MATMULS = 4
GROUPS = M // P

FLOPS = 2 * N * (D * M + D * R + R * M)


def tile_generalizedmatrix_kernel(tc, table, w, lf, ls, offs, out):
    nc = tc.nc
    with (
        tc.tile_pool(name="held", bufs=1) as held,
        tc.tile_pool(name="results", bufs=2 * GROUPS) as results,
        tc.psum_pool(name="warming", bufs=1) as warming,
    ):
        table_blocks = table.rearrange("(b p) d -> p b d", p=P)
        rows = [held.tile([P, BLOCKS_PER_LOAD, D], BF16, name=f"rows{c}") for c in range(LOADS)]
        for c in range(LOADS):
            queue = nc.sync if c % 2 == 0 else nc.scalar
            queue.dma_start(rows[c][:], table_blocks[:, c * BLOCKS_PER_LOAD : (c + 1) * BLOCKS_PER_LOAD, :])

        offsets = held.tile([P, N // 16], U16, name="offsets")
        nc.sync.dma_start(offsets[:], offs)

        lf_sb = held.tile([D, R], BF16, name="lf_sb")
        w_sb = held.tile([D, M], BF16, name="w_sb")
        ls_sb = held.tile([R, M], BF16, name="ls_sb")
        nc.sync.dma_start(lf_sb[:], lf)
        nc.sync.dma_start(w_sb[:], w)
        nc.scalar.dma_start(ls_sb[:], ls)

        identity = held.tile([P, P], BF16, name="identity")
        masks.make_identity(nc, identity[:])

        zeros = held.tile([P, N], BF16, name="zeros")
        nc.vector.memset(zeros[:], 0.0)
        unused = warming.tile([P, N], F32, name="unused")
        for i in range(WARMING_MATMULS):
            nc.tensor.matmul(unused[:], zeros[:, :P], zeros[:], start=True, stop=True)

        window = held.tile([D, S], BF16, name="window")
        with tc.psum_pool(name="flips", bufs=LOADS) as flips:
            for c in range(LOADS):
                flipped = flips.tile([D, BLOCKS_PER_LOAD * P], BF16, name="flipped")
                for k in range(BLOCKS_PER_LOAD):
                    nc.tensor.transpose(flipped[:, k * P : (k + 1) * P], rows[c][:, k, :], identity[:])
                columns = window[:, c * BLOCKS_PER_LOAD * P : (c + 1) * BLOCKS_PER_LOAD * P]
                if c % 2 == 0:
                    nc.vector.tensor_copy(columns, flipped[:])
                else:
                    nc.scalar.copy(columns, flipped[:])

        with tc.psum_pool(name="sums", bufs=1) as sums:
            h_sum = sums.tile([R, N], F32, name="h_sum")
            nc.tensor.matmul(h_sum[:], lf_sb[:], window[:].indirect(offsets[:]), start=True, stop=True)
            out_sums = [sums.tile([P, N], F32, name=f"out_sum{g}") for g in range(GROUPS)]
            for g in range(GROUPS):
                nc.tensor.matmul(
                    out_sums[g][:], w_sb[:, g * P : (g + 1) * P], window[:].indirect(offsets[:]), start=True, stop=False
                )

            h_sb = held.tile([R, N], BF16, name="h_sb")
            nc.vector.tensor_copy(h_sb[:], h_sum[:])

            for g in range(GROUPS):
                nc.tensor.matmul(out_sums[g][:], ls_sb[:, g * P : (g + 1) * P], h_sb[:], start=False, stop=True)
                for half in range(2):
                    columns = slice(half * N // 2, (half + 1) * N // 2)
                    result = results.tile([P, N // 2], F32, name="result")
                    if g % 2 == 0:
                        nc.vector.tensor_copy(result[:], out_sums[g][:, columns])
                    else:
                        nc.scalar.copy(result[:], out_sums[g][:, columns])
                    nc.sync.dma_start(out[g * P : (g + 1) * P, columns], result[:])
